import numpy as np
import ml_dtypes


def mxq(x, axis, fmt="e4m3"):
    dtype, down = {"e4m3": (ml_dtypes.float8_e4m3fn, 7), "e5m2": (ml_dtypes.float8_e5m2, 14)}[fmt]
    v = np.moveaxis(np.asarray(x, np.float32).astype(ml_dtypes.bfloat16).astype(np.float64), axis, -1)
    blocks = v.reshape(v.shape[:-1] + (-1, 32))
    amax = np.abs(blocks).max(-1, keepdims=True)
    byte = np.maximum(np.where(amax > 0, np.frexp(amax)[1] - 1 + 127, 0) - down, 1)
    scale = np.exp2(byte - 127.0)
    codes = (blocks / scale).astype(np.float32).astype(dtype).astype(np.float64)
    return np.moveaxis((codes * scale).reshape(v.shape), -1, axis)


WIDE = False


def mx_kscale(k):
    if not WIDE:
        return np.ones(k)
    levels = np.array([10, -10, 5, -5, 0])
    if k % 512:
        return np.exp2(np.random.permutation(np.resize(levels, k // 32))).repeat(32)
    a = np.empty((k // 512, 16))
    for p in range(k // 512):
        a[p, :8] = np.random.permutation(np.resize(levels, 8))
        for g in range(8):
            far = levels[np.abs(levels - a[p, g]) >= 10]
            a[p, g + 8] = far[np.random.randint(len(far))]
    return np.exp2(a.ravel()).repeat(32)


BF16 = ml_dtypes.bfloat16


def bf(x):
    return np.asarray(x, np.float32).astype(BF16)


def f64(x):
    return np.asarray(x).astype(np.float64)


B, N, SIZE, CH = 256, 16, 1024, 512


def sigmoid(v):
    return 1.0 / (1.0 + np.exp(-v))


def setup_inputs():
    s = mx_kscale(SIZE)
    half = np.concatenate([np.ones(CH), np.full(CH, 2.0 / np.sqrt(N))])
    return {"z_node": bf(np.random.standard_normal((B, N, SIZE)) * s),
            "z_children": bf(np.random.standard_normal((B, N, SIZE)) * half),
            "W_f": bf(np.random.standard_normal((CH, SIZE)) / np.sqrt(SIZE) / s),
            "U_f": bf(np.random.standard_normal((CH, CH)) / np.sqrt(CH)),
            "b_f": bf(np.random.standard_normal(CH) * 0.5)}


def core(z_node, z_children, W_f, U_f, b_f):
    h_k = f64(z_children)[..., :CH]
    c_k = f64(z_children)[..., CH:]
    f_j_k = sigmoid((mxq(f64(z_node), 2, "e4m3") @ mxq(f64(W_f), 1, "e4m3").T) + h_k @ f64(U_f).T + f64(b_f))
    return (f_j_k * c_k).sum(axis=1)


def e4m3fn_bytes(y):
    return np.clip(np.asarray(y, np.float64), -448.0, 448.0).astype(np.float32).astype(ml_dtypes.float8_e4m3fn).view(np.uint8)


def reference(z_node, z_children, W_f, U_f, b_f):
    out = core(z_node, z_children, W_f, U_f, b_f)
    s = np.max(np.abs(out), axis=-1, keepdims=True) / 448.0
    return out, e4m3fn_bytes(out / s)

@@ -1,0 +1,493 @@
+from contextlib import ExitStack
+
+import concourse.mybir as mybir
+from concourse.masks import make_identity
+
+B, N, SIZE, CH = 256, 16, 1024, 512
+FLOPS = 2 * B * N * CH * (SIZE + CH)
+
+F32 = mybir.dt.float32
+BF16 = mybir.dt.bfloat16
+U32 = mybir.dt.uint32
+U8 = mybir.dt.uint8
+FP8X4 = mybir.dt.float8_e4m3fn_x4
+FP8 = mybir.dt.float8_e4m3fn
+ALU = mybir.AluOpType
+ACT = mybir.ActivationFunctionType
+AX = mybir.AxisListType
+
+P = 128
+NG = 8
+NSTEP = 32
+LP = 4
+NWARM = (8, 2, 2)
+NB = {"zn": 8, "h": 8, "c": 8}
+FIRST_PERM = 16
+
+
+def tile_treelstm_pa_kernel(tc, z_node, z_children, W_f, U_f, b_f, out_0, out_1):
+    nc = tc.nc
+    with ExitStack() as ctx:
+        const = ctx.enter_context(tc.tile_pool(name="const", bufs=1))
+        raw = ctx.enter_context(tc.tile_pool(name="raw", bufs=1))
+        work = ctx.enter_context(tc.tile_pool(name="work", bufs=1))
+        psum = ctx.enter_context(tc.psum_pool(name="psum", bufs=1))
+        ctx.enter_context(tc.manual_schedule())
+
+        zn_v = z_node.rearrange("b n k -> (b n) k").rearrange("(g j r) k -> g r j k", g=NG, j=4)
+        zc_v = z_children.rearrange("b n k -> (b n) k").rearrange("(g j r) k -> g r j k", g=NG, j=4)
+        w_v = W_f.rearrange("(u p e) k -> u p e k", u=2, e=2)
+        u_v = U_f.rearrange("(u p e) k -> p u e k", u=2, e=2)
+        b_v = b_f.rearrange("(u p e) -> p u e", u=2, e=2)
+
+        bias_bf = const.tile([P, 2, 2], BF16, name="bias_bf")
+        nc.scalar.dma_start(out=bias_bf[:], in_=b_v)
+        zero = const.tile([P, 1], F32, name="zero")
+        nc.vector.memset(zero[:], 0.0)
+        wz = const.tile([P, 512], BF16, name="wz")
+        nc.vector.memset(wz[:], 0.0)
+        scr = const.tile([P, 1], F32, name="scr")
+        nc.scalar.activation(out=scr[:], in_=zero[:], func=ACT.Sigmoid)
+        ident = const.tile([P, P], F32, name="ident")
+        make_identity(nc, ident[:])
+        bias = const.tile([P, 4], F32, name="bias")
+
+        wcodes = const.tile([P, 2, 512], U32, name="wcodes", align_bytes=64)
+        wscales = const.tile([P, 2, 512], U8, name="wscales", align_bytes=64)
+        ut = const.tile([P, 4, 512], BF16, name="ut")
+        out_t = const.tile([P, 4, B], F32, name="out_t")
+        stat = const.tile([P, 8], F32, name="stat")
+
+        tiles = {}
+        emitted = {"zn": 0, "h": 0, "c": 0}
+        released = {"zn": 0, "h": 0, "c": 0}
+
+        def need(kind, i):
+            if kind == "u":
+                return -7
+            if kind == "w":
+                return -4 + i
+            if kind == "h":
+                return (-6.0, -6.0, -0.9, -0.8)[i] if i < 4 else 4 * (i // 2) - 8 + 2 * (i % 2)
+            if kind == "zn":
+                return (-2, -1, 0, 1)[i] if i < 4 else 2 * i - 6
+            return 4 * (i // 2) - 0.5
+
+        plan = [("u", 0), ("w", 0), ("w", 1)]
+        for i in range(2 * NG):
+            plan.extend([("zn", i), ("h", i), ("c", i)])
+        plan = sorted(plan, key=lambda e: need(e[0], e[1]))
+        plan_pos = [0]
+
+        def emit_load(kind, i):
+            jj = slice(2 * (i % 2), 2 * (i % 2) + 2)
+            if kind == "u":
+                t = raw.tile([P, 2, 2, CH], BF16, name="uraw")
+                nc.sync.dma_start(out=t[:], in_=u_v)
+            elif kind == "w":
+                t = raw.tile([P, 2, SIZE], BF16, name="wraw%d" % i, tag="wraw", bufs=2)
+                nc.sync.dma_start(out=t[:], in_=w_v[i])
+            elif kind == "zn":
+                t = raw.tile([P, 2, SIZE], BF16, name="zn%d" % i, tag="zn", bufs=NB["zn"])
+                nc.sync.dma_start(out=t[:], in_=zn_v[i // 2, :, jj, :])
+            elif kind == "h":
+                t = raw.tile([P, 2, CH], BF16, name="h%d" % i, tag="h", bufs=NB["h"])
+                nc.sync.dma_start(out=t[:], in_=zc_v[i // 2, :, jj, 0:CH])
+            else:
+                t = raw.tile([P, 2, CH], BF16, name="c%d" % i, tag="c", bufs=NB["c"])
+                nc.sync.dma_start(out=t[:], in_=zc_v[i // 2, :, jj, CH:2 * CH])
+            tiles[(kind, i)] = t
+
+        def pump():
+            while plan_pos[0] < len(plan):
+                kind, i = plan[plan_pos[0]]
+                if kind in NB:
+                    if emitted[kind] - released[kind] >= NB[kind]:
+                        return
+                    emitted[kind] += 1
+                emit_load(kind, i)
+                plan_pos[0] += 1
+
+        pump()
+
+        def emit_t(op):
+            nc.tensor.transpose(op[0], op[1], ident[:])
+
+        def warm(n):
+            if n > 0:
+                wp = psum.tile([P, 512], F32, name="warm", tag="p", bufs=2)
+                for i in range(n):
+                    nc.tensor.matmul(out=wp[:], lhsT=wz[:, 0:P], rhs=wz[:], start=True, stop=True)
+
+        def quarter_ops(src, g, name):
+            zt = psum.tile([P, 2, 2, P], F32, name=name, tag="zt", bufs=2)
+            words = src[:].bitcast(F32)
+            ops = []
+            for j2 in range(2):
+                for u2 in range(2):
+                    ops.append((zt[:, u2, j2, :], words[:, j2, 256 * g + u2:256 * (g + 1):2]))
+            return zt, ops
+
+        def copy_quarter(on_scalar, zt, name):
+            grp = work.tile([P, 512], F32, name=name, tag="grp", bufs=4, align_bytes=64)
+            o = grp[:].rearrange("p (c u) -> p c u", u=2)
+            i = zt[:].rearrange("p u j r -> p (j r) u")
+            if on_scalar:
+                nc.scalar.copy(out=o, in_=i)
+            else:
+                nc.vector.tensor_copy(out=o, in_=i)
+            return grp
+
+        def quantize(grp, codes, scales):
+            nc.vector.quantize_mx(out=codes.bitcast(FP8X4), scales=scales, in_=grp[:].bitcast(BF16))
+
+        zcodes = {}
+        zscales = {}
+
+        def z_dest(z):
+            gi, q = z // 4, z % 4
+            jp, g = q // 2, q % 2
+            key = (gi, g)
+            if key not in zcodes:
+                zcodes[key] = work.tile([P, 512], U32, name="zcd%d_%d" % key, tag="zcd", bufs=6, align_bytes=64)
+                zscales[key] = work.tile([P, 512], U8, name="zsc%d_%d" % key, tag="zsc", bufs=6, align_bytes=64)
+            sl = slice(256 * jp, 256 * jp + 256)
+            return zcodes[key][:, sl], zscales[key][:, sl]
+
+        perm_t = {}
+
+        def permute(i):
+            src = tiles[("zn", i)]
+            pt = raw.tile([P, 2, 2, 512], BF16, name="perm%d" % i, tag="perm", bufs=4)
+            perm_t[i] = pt
+            for j2 in range(2):
+                for g in range(2):
+                    nc.gpsimd.tensor_scalar(
+                        out=pt[:, j2, g, :].rearrange("r (u p e) -> r u p e", u=2, e=2),
+                        in0=src[:, j2, 512 * g:512 * g + 512].rearrange("r (p u e) -> r u p e", u=2, e=2),
+                        scalar1=1.0, scalar2=0.0, op0=ALU.mult, op1=ALU.add)
+
+        def z_ops(z):
+            i, g = z // 2, z % 2
+            if i < FIRST_PERM:
+                return quarter_ops(tiles[("zn", i)], g, "zt%d" % z)
+            zt = psum.tile([P, 2, 2, P], F32, name="zt%d" % z, tag="zt", bufs=2)
+            words = perm_t[i][:].bitcast(F32)
+            ops = []
+            for j2 in range(2):
+                for u2 in range(2):
+                    ops.append((zt[:, u2, j2, :], words[:, j2, g, 128 * u2:128 * u2 + 128]))
+            return zt, ops
+
+        ht_tiles = {}
+
+        def th_ops(gi, jp, tag, bufs):
+            ht = psum.tile([P, 2, 2, P], F32, name="ht%d_%d" % (gi, jp), tag=tag, bufs=bufs)
+            words = tiles[("h", 2 * gi + jp)][:].bitcast(F32)
+            ops = []
+            for j2 in range(2):
+                for uh in range(2):
+                    ops.append((ht[:, uh, j2, :], words[:, j2, 128 * uh:128 * uh + 128]))
+            return ht, ops
+
+        def copy_h(on_scalar, gi, jp, ht):
+            if gi not in ht_tiles:
+                ht_tiles[gi] = work.tile([P, 2, 512], F32, name="hT%d" % gi, tag="hT", bufs=3)
+            o = ht_tiles[gi][:, :, 256 * jp:256 * jp + 256]
+            i = ht[:].rearrange("p u j r -> p u (j r)")
+            if on_scalar:
+                nc.scalar.copy(out=o, in_=i)
+            else:
+                nc.vector.tensor_copy(out=o, in_=i)
+
+        ct_tiles = {}
+
+        def tc_ops(gi, u):
+            ct = psum.tile([P, 512], F32, name="ct%d_%d" % (gi, u), tag="ct", bufs=2)
+            ct_tiles[(gi, u)] = ct
+            ops = []
+            for j in range(4):
+                words = tiles[("c", 2 * gi + j // 2)][:].bitcast(F32)
+                ops.append((ct[:, 128 * j:128 * j + 128], words[:, j % 2, 128 * u:128 * u + 128]))
+            return ops
+
+        q_t, p_t, tmp_t, sum_t, f_t, g_t = {}, {}, {}, {}, {}, {}
+
+        def mx(s):
+            gi, m = s // 4, s % 4
+            q_t[s] = psum.tile([P, 512], F32, name="q%d" % s, tag="q", bufs=1)
+            for g in range(2):
+                nc.tensor.matmul_mx(
+                    out=q_t[s][:],
+                    lhsT=wcodes[:, g, 128 * m:128 * m + 128].bitcast(FP8X4),
+                    lhsT_scale=wscales[:, g, 128 * m:128 * m + 128],
+                    rhs=zcodes[(gi, g)][:].bitcast(FP8X4),
+                    rhs_scale=zscales[(gi, g)][:],
+                    start=(g == 0), stop=(g == 1))
+
+        def plain(s, kt):
+            gi, m = s // 4, s % 4
+            if kt == 0:
+                p_t[s] = psum.tile([P, 512], F32, name="p%d" % s, tag="p", bufs=2)
+            hb = ht_tiles[gi][:].bitcast(BF16).rearrange("p u (c e) -> p u c e", e=2)
+            nc.tensor.matmul(out=p_t[s][:], lhsT=ut[:, kt, 128 * m:128 * m + 128],
+                             rhs=hb[:, kt // 2, :, kt % 2], start=(kt == 0), stop=(kt == 3))
+
+        def weave(items, z_t, o_t):
+            nt = len(z_t) + len(o_t)
+            npl = len(items)
+            if npl < 2:
+                for it in items:
+                    plain(it[0], it[1])
+                for op in o_t + z_t:
+                    emit_t(op)
+                return
+            zi, oi, done = 0, 0, 0
+            for k in range(npl):
+                plain(items[k][0], items[k][1])
+                if k < npl - 1:
+                    goal = (nt * (k + 1) + npl - 2) // (npl - 1)
+                    first = True
+                    while done < goal:
+                        if (first and zi < len(z_t)) or oi >= len(o_t):
+                            emit_t(z_t[zi])
+                            zi += 1
+                        else:
+                            emit_t(o_t[oi])
+                            oi += 1
+                        first = False
+                        done += 1
+
+        def op_a(s):
+            tmp_t[s] = work.tile([P, 512], F32, name="tmp%d" % s, tag="tmp", bufs=6)
+            nc.scalar.copy(out=tmp_t[s][:], in_=p_t[s][:])
+
+        def op_b(s):
+            sum_t[s] = work.tile([P, 512], F32, name="sum%d" % s, tag="sum", bufs=3)
+            nc.vector.tensor_tensor(out=sum_t[s][:], in0=q_t[s][:], in1=tmp_t[s][:], op=ALU.add)
+
+        def op_sg(s):
+            m = s % 4
+            f_t[s] = work.tile([P, 512], F32, name="f%d" % s, tag="f", bufs=3)
+            nc.scalar.activation(out=f_t[s][:], in_=sum_t[s][:], func=ACT.Sigmoid, bias=bias[:, m:m + 1], scale=1.0)
+
+        def op_d(s):
+            gi, m = s // 4, s % 4
+            g_t[s] = work.tile([P, 512], F32, name="g%d" % s, tag="g", bufs=4)
+            cb = ct_tiles[(gi, m // 2)][:].bitcast(BF16).rearrange("p (x e) -> p x e", e=2)
+            nc.vector.tensor_tensor(out=g_t[s][:], in0=f_t[s][:], in1=cb[:, :, m % 2], op=ALU.mult)
+
+        def op_e(s):
+            gi, m = s // 4, s % 4
+            nc.vector.tensor_reduce(out=out_t[:, m, 32 * gi:32 * gi + 32],
+                                    in_=g_t[s][:].rearrange("c (q n) -> c q n", n=N),
+                                    axis=AX.X, op=ALU.add)
+
+        e2_t = {}
+
+        def op_tree(s):
+            g3 = g_t[s][:].rearrange("c (q n) -> c q n", n=N)
+            e1 = work.tile([P, 256], F32, name="e1_%d" % s, tag="e1", bufs=2)
+            e1v = e1[:].rearrange("c (q n) -> c q n", n=8)
+            nc.gpsimd.tensor_tensor(out=e1v, in0=g3[:, :, 0:8], in1=g3[:, :, 8:16], op=ALU.add)
+            if s % 2 == 0:
+                e2_t[s // 2] = work.tile([P, 2, P], F32, name="e2_%d" % s, tag="e2", bufs=3)
+            nc.gpsimd.tensor_tensor(out=e2_t[s // 2][:, s % 2, :].rearrange("c (q n) -> c q n", n=4),
+                                    in0=e1v[:, :, 0:4], in1=e1v[:, :, 4:8], op=ALU.add)
+
+        def op_e_pair(s):
+            gi, m = s // 4, s % 4
+            nc.vector.tensor_reduce(out=out_t[:, m:m + 2, 32 * gi:32 * gi + 32],
+                                    in_=e2_t[s // 2][:].rearrange("c a (q n) -> c a q n", n=4),
+                                    axis=AX.X, op=ALU.add)
+
+        osb_t, o8_t = {}, {}
+
+        def fin_t(h, u, tag, bufs):
+            ft = psum.tile([P, 2, P], F32, name="ft%d_%d" % (h, u), tag=tag, bufs=bufs)
+            for e in range(2):
+                nc.tensor.transpose(ft[:, e, :], out_t[:, 2 * u + e, 128 * h:128 * h + 128], ident[:])
+            return ft
+
+        def fin_copy(h, u, ft):
+            if h not in osb_t:
+                osb_t[h] = work.tile([P, CH], F32, name="osb%d" % h, tag="osb", bufs=2)
+            nc.scalar.copy(out=osb_t[h][:, 256 * u:256 * u + 256].rearrange("n (p e) -> n p e", e=2),
+                           in_=ft[:].rearrange("n e p -> n p e"))
+            if u == 1:
+                nc.sync.dma_start(out=out_0[128 * h:128 * h + 128, :], in_=osb_t[h][:])
+
+        def fin_amax(h, u):
+            nc.vector.tensor_reduce(out=stat[:, 4 * h + u:4 * h + u + 1], in_=osb_t[h][:, 256 * u:256 * u + 256],
+                                    axis=AX.X, op=ALU.max, apply_absolute_value=True)
+
+        def fin_scale(h):
+            nc.vector.tensor_scalar(out=stat[:, 4 * h + 2:4 * h + 3], in0=stat[:, 4 * h:4 * h + 1],
+                                    scalar1=stat[:, 4 * h + 1:4 * h + 2], scalar2=1.0 / 448.0,
+                                    op0=ALU.max, op1=ALU.mult)
+            nc.vector.reciprocal(out=stat[:, 4 * h + 3:4 * h + 4], in_=stat[:, 4 * h + 2:4 * h + 3])
+
+        def fin_cast(h, vcols):
+            o8_t[h] = work.tile([P, CH], FP8, name="o8_%d" % h, tag="o8", bufs=2)
+            r = stat[:, 4 * h + 3:4 * h + 4]
+            if vcols > 0:
+                nc.vector.tensor_scalar(out=o8_t[h][:, 0:vcols], in0=osb_t[h][:, 0:vcols], scalar1=r, scalar2=None,
+                                        op0=ALU.mult, saturate=False)
+            if vcols < CH:
+                nc.scalar.activation(out=o8_t[h][:, vcols:CH], in_=osb_t[h][:, vcols:CH], func=ACT.Identity,
+                                     scale=r, bias=zero[:, 0:1], saturate=False)
+            nc.sync.dma_start(out=out_1[128 * h:128 * h + 128, :], in_=o8_t[h][:].bitcast(U8))
+
+        warm(NWARM[0])
+        uwords = tiles[("u", 0)][:].bitcast(F32)
+        ups = []
+        for uh in range(2):
+            up = psum.tile([P, 4, P], F32, name="up%d" % uh, tag="ct", bufs=2)
+            for m in range(4):
+                nc.tensor.transpose(up[:, m, :], uwords[:, m // 2, m % 2, 128 * uh:128 * uh + 128], ident[:])
+            ups.append(up)
+        for uh in range(2):
+            v = ups[uh][:].rearrange("p m c -> p (m c)").bitcast(BF16).rearrange("p (x e) -> p e x", e=2)
+            if uh == 0:
+                nc.vector.tensor_copy(out=ut[:, 0:2, :], in_=v)
+            else:
+                nc.scalar.copy(out=ut[:, 2:4, :], in_=v)
+        warm(NWARM[1])
+        ht_a, ops_a = th_ops(0, 0, "ht", 1)
+        for op in ops_a:
+            emit_t(op)
+        ht_b, ops_b = th_ops(0, 1, "q", 1)
+        for op in ops_b:
+            emit_t(op)
+        copy_h(True, 0, 0, ht_a)
+        copy_h(False, 0, 1, ht_b)
+        released["h"] += 2
+        warm(NWARM[2])
+        nc.vector.tensor_copy(out=bias[:], in_=bias_bf[:].rearrange("p u e -> p (u e)"))
+
+        pro = []
+        for u in range(2):
+            for g in range(2):
+                pro.append((("w", u), g, wcodes[:, g, 256 * u:256 * u + 256], wscales[:, g, 256 * u:256 * u + 256]))
+        for z in range(4):
+            cd, sc = z_dest(z)
+            pro.append((("zn", z // 2), z % 2, cd, sc))
+        qz_list = []
+        for pu in range(LP):
+            z_t = []
+            o_t = []
+            zts = []
+            for k in (2 * pu, 2 * pu + 1):
+                zt, ops = quarter_ops(tiles[pro[k][0]], pro[k][1], "pzt%d" % k)
+                zts.append((k, zt))
+                z_t.extend(ops)
+            ht10 = None
+            if pu == LP - 1:
+                ht10, o_t = th_ops(1, 0, "q", 1)
+            weave([(pu, kt) for kt in range(4)], z_t + o_t, [])
+            if pu >= 1:
+                op_a(pu - 1)
+            for item in qz_list:
+                quantize(*item)
+            qz_list.clear()
+            for n_, (k, zt) in enumerate(zts):
+                grp = copy_quarter(n_ == 0, zt, "pgrp%d" % k)
+                qz_list.append((grp, pro[k][2], pro[k][3]))
+            if pu >= 2:
+                released["zn"] += 1
+            if ht10 is not None:
+                copy_h(True, 1, 0, ht10)
+                released["h"] += 1
+        ht11, ops = th_ops(1, 1, "ht", 1)
+        for op in ops:
+            emit_t(op)
+        for op in tc_ops(0, 0):
+            emit_t(op)
+        for item in qz_list:
+            quantize(*item)
+        qz_list.clear()
+        copy_h(True, 1, 1, ht11)
+        released["h"] += 1
+        pump()
+
+        zt_list = []
+        stream = [(u, kt) for u in range(LP, NSTEP) for kt in range(4)]
+        spos = 0
+        a_list = [LP - 1]
+        for s in range(NSTEP):
+            mx(s)
+            for u in a_list:
+                op_a(u)
+            a_list.clear()
+            if s >= 1:
+                op_sg(s - 1)
+            qz_now = list(qz_list)
+            qz_list.clear()
+            for n_, (z, zt) in enumerate(zt_list):
+                grp = copy_quarter(n_ == 0, zt, "grp%d" % z)
+                cd, sc = z_dest(z)
+                qz_list.append((grp, cd, sc))
+            zt_list.clear()
+            for item in qz_now:
+                quantize(*item)
+            if s >= 4 and s % 2 == 0:
+                op_e_pair(s - 4)
+            if s == NSTEP - 1:
+                op_e_pair(s - 3)
+            op_b(s)
+            if s >= 1:
+                op_d(s - 1)
+                if s - 1 < NSTEP - 2:
+                    op_tree(s - 1)
+            z_t = []
+            zl = ((4, 5), (6, 7))[s] if s < 2 else ((s + 6,) if s + 6 < NSTEP else ())
+            for z in zl:
+                zt, ops = z_ops(z)
+                zt_list.append((z, zt))
+                z_t.extend(ops)
+            o_t = []
+            ht = None
+            gi, jp = (s + 8) // 4, ((s + 8) % 4) // 2
+            if s % 2 == 0 and gi < NG:
+                ht, o_t = th_ops(gi, jp, "ht", 1)
+            gc, uc = (s + 1) // 4, ((s + 1) % 4) // 2
+            if s % 2 == 1 and gc < NG:
+                o_t = tc_ops(gc, uc)
+            upto = min(len(stream), (len(stream) * (s + 1) + NSTEP - 2) // (NSTEP - 1))
+            items = stream[spos:upto]
+            spos = upto
+            weave(items, z_t, o_t)
+            for it in items:
+                if it[1] == 3:
+                    a_list.append(it[0])
+            if ht is not None:
+                copy_h(jp == 0, gi, jp, ht)
+                released["h"] += 1
+            for z in zl:
+                if z % 2 == 1:
+                    released["zn"] += 1
+            if s % 2 == 1 and gc < NG and uc == 1:
+                released["c"] += 2
+            pump()
+
+        last = NSTEP - 1
+        ft00 = fin_t(0, 0, "zt", 2)
+        ft01 = fin_t(0, 1, "zt", 2)
+        ft10 = fin_t(1, 0, "ht", 1)
+        op_sg(last)
+        op_e(last - 1)
+        fin_copy(0, 0, ft00)
+        fin_copy(0, 1, ft01)
+        fin_copy(1, 0, ft10)
+        op_d(last)
+        fin_amax(0, 0)
+        op_e(last)
+        ft11 = fin_t(1, 1, "ct", 2)
+        fin_copy(1, 1, ft11)
+        fin_amax(0, 1)
+        fin_scale(0)
+        fin_amax(1, 0)
+        fin_cast(0, 0)
+        fin_amax(1, 1)
+        fin_scale(1)
+        fin_cast(1, 256)

@@ -19,7 +19,7 @@ AX = mybir.AxisListType
 P = 128
 NG = 8
 NSTEP = 32
-LP = 4
+LP = 2
 NWARM = (8, 2, 2)
 NB = {"zn": 8, "h": 8, "c": 8}
 FIRST_PERM = 16
@@ -119,8 +119,8 @@ def tile_treelstm_pa_kernel(tc, z_node, z_children, W_f, U_f, b_f, out_0, out_1)
                 for i in range(n):
                     nc.tensor.matmul(out=wp[:], lhsT=wz[:, 0:P], rhs=wz[:], start=True, stop=True)
 
-        def quarter_ops(src, g, name):
-            zt = psum.tile([P, 2, 2, P], F32, name=name, tag="zt", bufs=2)
+        def quarter_ops(src, g, name, tag="zt"):
+            zt = psum.tile([P, 2, 2, P], F32, name=name, tag=tag, bufs=2)
             words = src[:].bitcast(F32)
             ops = []
             for j2 in range(2):
@@ -297,9 +297,12 @@ def tile_treelstm_pa_kernel(tc, z_node, z_children, W_f, U_f, b_f, out_0, out_1)
 
         def op_e_pair(s):
             gi, m = s // 4, s % 4
-            nc.vector.tensor_reduce(out=out_t[:, m:m + 2, 32 * gi:32 * gi + 32],
-                                    in_=e2_t[s // 2][:].rearrange("c a (q n) -> c a q n", n=4),
-                                    axis=AX.X, op=ALU.add)
+            e2v = e2_t[s // 2][:].rearrange("c a (q n) -> c a q n", n=4)
+            e3 = work.tile([P, 2, 64], F32, name="e3_%d" % s, tag="e3", bufs=2)
+            e3v = e3[:].rearrange("c a (q n) -> c a q n", n=2)
+            nc.gpsimd.tensor_tensor(out=e3v, in0=e2v[:, :, :, 0:2], in1=e2v[:, :, :, 2:4], op=ALU.add)
+            nc.gpsimd.tensor_tensor(out=out_t[:, m:m + 2, 32 * gi:32 * gi + 32], in0=e3v[:, :, :, 0],
+                                    in1=e3v[:, :, :, 1], op=ALU.add)
 
         osb_t, o8_t = {}, {}
 
@@ -375,29 +378,24 @@ def tile_treelstm_pa_kernel(tc, z_node, z_children, W_f, U_f, b_f, out_0, out_1)
         qz_list = []
         for pu in range(LP):
             z_t = []
-            o_t = []
             zts = []
-            for k in (2 * pu, 2 * pu + 1):
-                zt, ops = quarter_ops(tiles[pro[k][0]], pro[k][1], "pzt%d" % k)
+            for k in range(4 * pu, 4 * pu + 4):
+                zt, ops = quarter_ops(tiles[pro[k][0]], pro[k][1], "pzt%d" % k, ("zt", "ct")[(k % 4) // 2])
                 zts.append((k, zt))
                 z_t.extend(ops)
-            ht10 = None
-            if pu == LP - 1:
-                ht10, o_t = th_ops(1, 0, "q", 1)
-            weave([(pu, kt) for kt in range(4)], z_t + o_t, [])
+            weave([(pu, kt) for kt in range(4)], z_t, [])
             if pu >= 1:
                 op_a(pu - 1)
             for item in qz_list:
                 quantize(*item)
             qz_list.clear()
             for n_, (k, zt) in enumerate(zts):
-                grp = copy_quarter(n_ == 0, zt, "pgrp%d" % k)
+                grp = copy_quarter(n_ % 2 == 0, zt, "pgrp%d" % k)
                 qz_list.append((grp, pro[k][2], pro[k][3]))
-            if pu >= 2:
-                released["zn"] += 1
-            if ht10 is not None:
-                copy_h(True, 1, 0, ht10)
-                released["h"] += 1
+        released["zn"] += 2
+        ht10, ops = th_ops(1, 0, "q", 1)
+        for op in ops:
+            emit_t(op)
         ht11, ops = th_ops(1, 1, "ht", 1)
         for op in ops:
             emit_t(op)
@@ -406,8 +404,9 @@ def tile_treelstm_pa_kernel(tc, z_node, z_children, W_f, U_f, b_f, out_0, out_1)
         for item in qz_list:
             quantize(*item)
         qz_list.clear()
+        copy_h(True, 1, 0, ht10)
         copy_h(True, 1, 1, ht11)
-        released["h"] += 1
+        released["h"] += 2
         pump()
 
         zt_list = []
@@ -461,7 +460,7 @@ def tile_treelstm_pa_kernel(tc, z_node, z_children, W_f, U_f, b_f, out_0, out_1)
                 if it[1] == 3:
                     a_list.append(it[0])
             if ht is not None:
-                copy_h(jp == 0, gi, jp, ht)
+                copy_h(False, gi, jp, ht)
                 released["h"] += 1
             for z in zl:
                 if z % 2 == 1:

@@ -19,7 +19,7 @@ AX = mybir.AxisListType
 P = 128
 NG = 8
 NSTEP = 32
-LP = 2
+LP = 3
 NWARM = (8, 2, 2)
 NB = {"zn": 8, "h": 8, "c": 8}
 FIRST_PERM = 16
@@ -376,7 +376,7 @@ def tile_treelstm_pa_kernel(tc, z_node, z_children, W_f, U_f, b_f, out_0, out_1)
             cd, sc = z_dest(z)
             pro.append((("zn", z // 2), z % 2, cd, sc))
         qz_list = []
-        for pu in range(LP):
+        for pu in range(2):
             z_t = []
             zts = []
             for k in range(4 * pu, 4 * pu + 4):
@@ -393,14 +393,10 @@ def tile_treelstm_pa_kernel(tc, z_node, z_children, W_f, U_f, b_f, out_0, out_1)
                 grp = copy_quarter(n_ % 2 == 0, zt, "pgrp%d" % k)
                 qz_list.append((grp, pro[k][2], pro[k][3]))
         released["zn"] += 2
-        ht10, ops = th_ops(1, 0, "q", 1)
-        for op in ops:
-            emit_t(op)
-        ht11, ops = th_ops(1, 1, "ht", 1)
-        for op in ops:
-            emit_t(op)
-        for op in tc_ops(0, 0):
-            emit_t(op)
+        ht10, ops10 = th_ops(1, 0, "q", 1)
+        ht11, ops11 = th_ops(1, 1, "ht", 1)
+        weave([(2, kt) for kt in range(4)], ops10 + ops11 + tc_ops(0, 0), [])
+        op_a(1)
         for item in qz_list:
             quantize(*item)
         qz_list.clear()

@@ -423,13 +423,13 @@ def tile_treelstm_pa_kernel(tc, z_node, z_children, W_f, U_f, b_f, out_0, out_1)
                 cd, sc = z_dest(z)
                 qz_list.append((grp, cd, sc))
             zt_list.clear()
-            for item in qz_now:
-                quantize(*item)
             if s >= 4 and s % 2 == 0:
                 op_e_pair(s - 4)
             if s == NSTEP - 1:
                 op_e_pair(s - 3)
             op_b(s)
+            for item in qz_now:
+                quantize(*item)
             if s >= 1:
                 op_d(s - 1)
                 if s - 1 < NSTEP - 2:

@@ -452,6 +452,12 @@ def tile_treelstm_pa_kernel(tc, z_node, z_children, W_f, U_f, b_f, out_0, out_1)
             items = stream[spos:upto]
             spos = upto
             weave(items, z_t, o_t)
+            if s < 2:
+                for n_, (z, zt) in enumerate(zt_list):
+                    grp = copy_quarter(n_ == 0, zt, "grp%d" % z)
+                    cd, sc = z_dest(z)
+                    qz_list.append((grp, cd, sc))
+                zt_list.clear()
             for it in items:
                 if it[1] == 3:
                     a_list.append(it[0])

@@ -68,10 +68,10 @@ def tile_treelstm_pa_kernel(tc, z_node, z_children, W_f, U_f, b_f, out_0, out_1)
             if kind == "w":
                 return -4 + i
             if kind == "h":
-                return (-6.0, -6.0, -0.9, -0.8)[i] if i < 4 else 4 * (i // 2) - 8 + 2 * (i % 2)
+                return (-6.0, -6.0, -0.9, -0.8)[i] if i < 4 else 4 * (i // 2) - 6 + 2 * (i % 2)
             if kind == "zn":
                 return (-2, -1, 0, 1)[i] if i < 4 else 2 * i - 6
-            return 4 * (i // 2) - 0.5
+            return 4 * (i // 2) - 0.5 if i >= 2 else 0.5
 
         plan = [("u", 0), ("w", 0), ("w", 1)]
         for i in range(2 * NG):
@@ -395,7 +395,7 @@ def tile_treelstm_pa_kernel(tc, z_node, z_children, W_f, U_f, b_f, out_0, out_1)
         released["zn"] += 2
         ht10, ops10 = th_ops(1, 0, "q", 1)
         ht11, ops11 = th_ops(1, 1, "ht", 1)
-        weave([(2, kt) for kt in range(4)], ops10 + ops11 + tc_ops(0, 0), [])
+        weave([(2, kt) for kt in range(4)], ops10 + ops11, [])
         op_a(1)
         for item in qz_list:
             quantize(*item)
@@ -442,12 +442,14 @@ def tile_treelstm_pa_kernel(tc, z_node, z_children, W_f, U_f, b_f, out_0, out_1)
                 z_t.extend(ops)
             o_t = []
             ht = None
-            gi, jp = (s + 8) // 4, ((s + 8) % 4) // 2
-            if s % 2 == 0 and gi < NG:
+            gi, jp = (s + 6) // 4, ((s + 6) % 4) // 2
+            if s % 2 == 0 and 2 <= gi < NG:
                 ht, o_t = th_ops(gi, jp, "ht", 1)
             gc, uc = (s + 1) // 4, ((s + 1) % 4) // 2
             if s % 2 == 1 and gc < NG:
                 o_t = tc_ops(gc, uc)
+            if s == 0:
+                o_t = tc_ops(0, 0)
             upto = min(len(stream), (len(stream) * (s + 1) + NSTEP - 2) // (NSTEP - 1))
             items = stream[spos:upto]
             spos = upto

@@ -449,7 +449,7 @@ def tile_treelstm_pa_kernel(tc, z_node, z_children, W_f, U_f, b_f, out_0, out_1)
             if s % 2 == 1 and gc < NG:
                 o_t = tc_ops(gc, uc)
             if s == 0:
-                o_t = tc_ops(0, 0)
+                z_t.extend(tc_ops(0, 0))
             upto = min(len(stream), (len(stream) * (s + 1) + NSTEP - 2) // (NSTEP - 1))
             items = stream[spos:upto]
             spos = upto

from contextlib import ExitStack

import concourse.mybir as mybir
from concourse.masks import make_identity

B, N, SIZE, CH = 256, 16, 1024, 512
FLOPS = 2 * B * N * CH * (SIZE + CH)

F32 = mybir.dt.float32
BF16 = mybir.dt.bfloat16
U32 = mybir.dt.uint32
U8 = mybir.dt.uint8
FP8X4 = mybir.dt.float8_e4m3fn_x4
FP8 = mybir.dt.float8_e4m3fn
ALU = mybir.AluOpType
ACT = mybir.ActivationFunctionType
AX = mybir.AxisListType

P = 128
NG = 8
NSTEP = 32
LP = 3
NWARM = (8, 2, 2)
NB = {"zn": 8, "h": 8, "c": 8}
FIRST_PERM = 16


def tile_treelstm_pa_kernel(tc, z_node, z_children, W_f, U_f, b_f, out_0, out_1):
    nc = tc.nc
    with ExitStack() as ctx:
        const = ctx.enter_context(tc.tile_pool(name="const", bufs=1))
        raw = ctx.enter_context(tc.tile_pool(name="raw", bufs=1))
        work = ctx.enter_context(tc.tile_pool(name="work", bufs=1))
        psum = ctx.enter_context(tc.psum_pool(name="psum", bufs=1))
        ctx.enter_context(tc.manual_schedule())

        zn_v = z_node.rearrange("b n k -> (b n) k").rearrange("(g j r) k -> g r j k", g=NG, j=4)
        zc_v = z_children.rearrange("b n k -> (b n) k").rearrange("(g j r) k -> g r j k", g=NG, j=4)
        w_v = W_f.rearrange("(u p e) k -> u p e k", u=2, e=2)
        u_v = U_f.rearrange("(u p e) k -> p u e k", u=2, e=2)
        b_v = b_f.rearrange("(u p e) -> p u e", u=2, e=2)

        bias_bf = const.tile([P, 2, 2], BF16, name="bias_bf")
        nc.scalar.dma_start(out=bias_bf[:], in_=b_v)
        zero = const.tile([P, 1], F32, name="zero")
        nc.vector.memset(zero[:], 0.0)
        wz = const.tile([P, 512], BF16, name="wz")
        nc.vector.memset(wz[:], 0.0)
        scr = const.tile([P, 1], F32, name="scr")
        nc.scalar.activation(out=scr[:], in_=zero[:], func=ACT.Sigmoid)
        ident = const.tile([P, P], F32, name="ident")
        make_identity(nc, ident[:])
        bias = const.tile([P, 4], F32, name="bias")

        wcodes = const.tile([P, 2, 512], U32, name="wcodes", align_bytes=64)
        wscales = const.tile([P, 2, 512], U8, name="wscales", align_bytes=64)
        ut = const.tile([P, 4, 512], BF16, name="ut")
        out_t = const.tile([P, 4, B], F32, name="out_t")
        stat = const.tile([P, 8], F32, name="stat")

        tiles = {}
        emitted = {"zn": 0, "h": 0, "c": 0}
        released = {"zn": 0, "h": 0, "c": 0}

        def need(kind, i):
            if kind == "u":
                return -7
            if kind == "w":
                return -4 + i
            if kind == "h":
                return (-6.0, -6.0, -0.9, -0.8)[i] if i < 4 else 4 * (i // 2) - 6 + 2 * (i % 2)
            if kind == "zn":
                return (-2, -1, 0, 1)[i] if i < 4 else 2 * i - 6
            return 4 * (i // 2) - 0.5 if i >= 2 else 0.5

        plan = [("u", 0), ("w", 0), ("w", 1)]
        for i in range(2 * NG):
            plan.extend([("zn", i), ("h", i), ("c", i)])
        plan = sorted(plan, key=lambda e: need(e[0], e[1]))
        plan_pos = [0]

        def emit_load(kind, i):
            jj = slice(2 * (i % 2), 2 * (i % 2) + 2)
            if kind == "u":
                t = raw.tile([P, 2, 2, CH], BF16, name="uraw")
                nc.sync.dma_start(out=t[:], in_=u_v)
            elif kind == "w":
                t = raw.tile([P, 2, SIZE], BF16, name="wraw%d" % i, tag="wraw", bufs=2)
                nc.sync.dma_start(out=t[:], in_=w_v[i])
            elif kind == "zn":
                t = raw.tile([P, 2, SIZE], BF16, name="zn%d" % i, tag="zn", bufs=NB["zn"])
                nc.sync.dma_start(out=t[:], in_=zn_v[i // 2, :, jj, :])
            elif kind == "h":
                t = raw.tile([P, 2, CH], BF16, name="h%d" % i, tag="h", bufs=NB["h"])
                nc.sync.dma_start(out=t[:], in_=zc_v[i // 2, :, jj, 0:CH])
            else:
                t = raw.tile([P, 2, CH], BF16, name="c%d" % i, tag="c", bufs=NB["c"])
                nc.sync.dma_start(out=t[:], in_=zc_v[i // 2, :, jj, CH:2 * CH])
            tiles[(kind, i)] = t

        def pump():
            while plan_pos[0] < len(plan):
                kind, i = plan[plan_pos[0]]
                if kind in NB:
                    if emitted[kind] - released[kind] >= NB[kind]:
                        return
                    emitted[kind] += 1
                emit_load(kind, i)
                plan_pos[0] += 1

        pump()

        def emit_t(op):
            nc.tensor.transpose(op[0], op[1], ident[:])

        def warm(n):
            if n > 0:
                wp = psum.tile([P, 512], F32, name="warm", tag="p", bufs=2)
                for i in range(n):
                    nc.tensor.matmul(out=wp[:], lhsT=wz[:, 0:P], rhs=wz[:], start=True, stop=True)

        def quarter_ops(src, g, name, tag="zt"):
            zt = psum.tile([P, 2, 2, P], F32, name=name, tag=tag, bufs=2)
            words = src[:].bitcast(F32)
            ops = []
            for j2 in range(2):
                for u2 in range(2):
                    ops.append((zt[:, u2, j2, :], words[:, j2, 256 * g + u2:256 * (g + 1):2]))
            return zt, ops

        def copy_quarter(on_scalar, zt, name):
            grp = work.tile([P, 512], F32, name=name, tag="grp", bufs=4, align_bytes=64)
            o = grp[:].rearrange("p (c u) -> p c u", u=2)
            i = zt[:].rearrange("p u j r -> p (j r) u")
            if on_scalar:
                nc.scalar.copy(out=o, in_=i)
            else:
                nc.vector.tensor_copy(out=o, in_=i)
            return grp

        def quantize(grp, codes, scales):
            nc.vector.quantize_mx(out=codes.bitcast(FP8X4), scales=scales, in_=grp[:].bitcast(BF16))

        zcodes = {}
        zscales = {}

        def z_dest(z):
            gi, q = z // 4, z % 4
            jp, g = q // 2, q % 2
            key = (gi, g)
            if key not in zcodes:
                zcodes[key] = work.tile([P, 512], U32, name="zcd%d_%d" % key, tag="zcd", bufs=6, align_bytes=64)
                zscales[key] = work.tile([P, 512], U8, name="zsc%d_%d" % key, tag="zsc", bufs=6, align_bytes=64)
            sl = slice(256 * jp, 256 * jp + 256)
            return zcodes[key][:, sl], zscales[key][:, sl]

        perm_t = {}

        def permute(i):
            src = tiles[("zn", i)]
            pt = raw.tile([P, 2, 2, 512], BF16, name="perm%d" % i, tag="perm", bufs=4)
            perm_t[i] = pt
            for j2 in range(2):
                for g in range(2):
                    nc.gpsimd.tensor_scalar(
                        out=pt[:, j2, g, :].rearrange("r (u p e) -> r u p e", u=2, e=2),
                        in0=src[:, j2, 512 * g:512 * g + 512].rearrange("r (p u e) -> r u p e", u=2, e=2),
                        scalar1=1.0, scalar2=0.0, op0=ALU.mult, op1=ALU.add)

        def z_ops(z):
            i, g = z // 2, z % 2
            if i < FIRST_PERM:
                return quarter_ops(tiles[("zn", i)], g, "zt%d" % z)
            zt = psum.tile([P, 2, 2, P], F32, name="zt%d" % z, tag="zt", bufs=2)
            words = perm_t[i][:].bitcast(F32)
            ops = []
            for j2 in range(2):
                for u2 in range(2):
                    ops.append((zt[:, u2, j2, :], words[:, j2, g, 128 * u2:128 * u2 + 128]))
            return zt, ops

        ht_tiles = {}

        def th_ops(gi, jp, tag, bufs):
            ht = psum.tile([P, 2, 2, P], F32, name="ht%d_%d" % (gi, jp), tag=tag, bufs=bufs)
            words = tiles[("h", 2 * gi + jp)][:].bitcast(F32)
            ops = []
            for j2 in range(2):
                for uh in range(2):
                    ops.append((ht[:, uh, j2, :], words[:, j2, 128 * uh:128 * uh + 128]))
            return ht, ops

        def copy_h(on_scalar, gi, jp, ht):
            if gi not in ht_tiles:
                ht_tiles[gi] = work.tile([P, 2, 512], F32, name="hT%d" % gi, tag="hT", bufs=3)
            o = ht_tiles[gi][:, :, 256 * jp:256 * jp + 256]
            i = ht[:].rearrange("p u j r -> p u (j r)")
            if on_scalar:
                nc.scalar.copy(out=o, in_=i)
            else:
                nc.vector.tensor_copy(out=o, in_=i)

        ct_tiles = {}

        def tc_ops(gi, u):
            ct = psum.tile([P, 512], F32, name="ct%d_%d" % (gi, u), tag="ct", bufs=2)
            ct_tiles[(gi, u)] = ct
            ops = []
            for j in range(4):
                words = tiles[("c", 2 * gi + j // 2)][:].bitcast(F32)
                ops.append((ct[:, 128 * j:128 * j + 128], words[:, j % 2, 128 * u:128 * u + 128]))
            return ops

        q_t, p_t, tmp_t, sum_t, f_t, g_t = {}, {}, {}, {}, {}, {}

        def mx(s):
            gi, m = s // 4, s % 4
            q_t[s] = psum.tile([P, 512], F32, name="q%d" % s, tag="q", bufs=1)
            for g in range(2):
                nc.tensor.matmul_mx(
                    out=q_t[s][:],
                    lhsT=wcodes[:, g, 128 * m:128 * m + 128].bitcast(FP8X4),
                    lhsT_scale=wscales[:, g, 128 * m:128 * m + 128],
                    rhs=zcodes[(gi, g)][:].bitcast(FP8X4),
                    rhs_scale=zscales[(gi, g)][:],
                    start=(g == 0), stop=(g == 1))

        def plain(s, kt):
            gi, m = s // 4, s % 4
            if kt == 0:
                p_t[s] = psum.tile([P, 512], F32, name="p%d" % s, tag="p", bufs=2)
            hb = ht_tiles[gi][:].bitcast(BF16).rearrange("p u (c e) -> p u c e", e=2)
            nc.tensor.matmul(out=p_t[s][:], lhsT=ut[:, kt, 128 * m:128 * m + 128],
                             rhs=hb[:, kt // 2, :, kt % 2], start=(kt == 0), stop=(kt == 3))

        def weave(items, z_t, o_t):
            nt = len(z_t) + len(o_t)
            npl = len(items)
            if npl < 2:
                for it in items:
                    plain(it[0], it[1])
                for op in o_t + z_t:
                    emit_t(op)
                return
            zi, oi, done = 0, 0, 0
            for k in range(npl):
                plain(items[k][0], items[k][1])
                if k < npl - 1:
                    goal = (nt * (k + 1) + npl - 2) // (npl - 1)
                    first = True
                    while done < goal:
                        if (first and zi < len(z_t)) or oi >= len(o_t):
                            emit_t(z_t[zi])
                            zi += 1
                        else:
                            emit_t(o_t[oi])
                            oi += 1
                        first = False
                        done += 1

        def op_a(s):
            tmp_t[s] = work.tile([P, 512], F32, name="tmp%d" % s, tag="tmp", bufs=6)
            nc.scalar.copy(out=tmp_t[s][:], in_=p_t[s][:])

        def op_b(s):
            sum_t[s] = work.tile([P, 512], F32, name="sum%d" % s, tag="sum", bufs=3)
            nc.vector.tensor_tensor(out=sum_t[s][:], in0=q_t[s][:], in1=tmp_t[s][:], op=ALU.add)

        def op_sg(s):
            m = s % 4
            f_t[s] = work.tile([P, 512], F32, name="f%d" % s, tag="f", bufs=3)
            nc.scalar.activation(out=f_t[s][:], in_=sum_t[s][:], func=ACT.Sigmoid, bias=bias[:, m:m + 1], scale=1.0)

        def op_d(s):
            gi, m = s // 4, s % 4
            g_t[s] = work.tile([P, 512], F32, name="g%d" % s, tag="g", bufs=4)
            cb = ct_tiles[(gi, m // 2)][:].bitcast(BF16).rearrange("p (x e) -> p x e", e=2)
            nc.vector.tensor_tensor(out=g_t[s][:], in0=f_t[s][:], in1=cb[:, :, m % 2], op=ALU.mult)

        def op_e(s):
            gi, m = s // 4, s % 4
            nc.vector.tensor_reduce(out=out_t[:, m, 32 * gi:32 * gi + 32],
                                    in_=g_t[s][:].rearrange("c (q n) -> c q n", n=N),
                                    axis=AX.X, op=ALU.add)

        e2_t = {}

        def op_tree(s):
            g3 = g_t[s][:].rearrange("c (q n) -> c q n", n=N)
            e1 = work.tile([P, 256], F32, name="e1_%d" % s, tag="e1", bufs=2)
            e1v = e1[:].rearrange("c (q n) -> c q n", n=8)
            nc.gpsimd.tensor_tensor(out=e1v, in0=g3[:, :, 0:8], in1=g3[:, :, 8:16], op=ALU.add)
            if s % 2 == 0:
                e2_t[s // 2] = work.tile([P, 2, P], F32, name="e2_%d" % s, tag="e2", bufs=3)
            nc.gpsimd.tensor_tensor(out=e2_t[s // 2][:, s % 2, :].rearrange("c (q n) -> c q n", n=4),
                                    in0=e1v[:, :, 0:4], in1=e1v[:, :, 4:8], op=ALU.add)

        def op_e_pair(s):
            gi, m = s // 4, s % 4
            e2v = e2_t[s // 2][:].rearrange("c a (q n) -> c a q n", n=4)
            e3 = work.tile([P, 2, 64], F32, name="e3_%d" % s, tag="e3", bufs=2)
            e3v = e3[:].rearrange("c a (q n) -> c a q n", n=2)
            nc.gpsimd.tensor_tensor(out=e3v, in0=e2v[:, :, :, 0:2], in1=e2v[:, :, :, 2:4], op=ALU.add)
            nc.gpsimd.tensor_tensor(out=out_t[:, m:m + 2, 32 * gi:32 * gi + 32], in0=e3v[:, :, :, 0],
                                    in1=e3v[:, :, :, 1], op=ALU.add)

        osb_t, o8_t = {}, {}

        def fin_t(h, u, tag, bufs):
            ft = psum.tile([P, 2, P], F32, name="ft%d_%d" % (h, u), tag=tag, bufs=bufs)
            for e in range(2):
                nc.tensor.transpose(ft[:, e, :], out_t[:, 2 * u + e, 128 * h:128 * h + 128], ident[:])
            return ft

        def fin_copy(h, u, ft):
            if h not in osb_t:
                osb_t[h] = work.tile([P, CH], F32, name="osb%d" % h, tag="osb", bufs=2)
            nc.scalar.copy(out=osb_t[h][:, 256 * u:256 * u + 256].rearrange("n (p e) -> n p e", e=2),
                           in_=ft[:].rearrange("n e p -> n p e"))
            if u == 1:
                nc.sync.dma_start(out=out_0[128 * h:128 * h + 128, :], in_=osb_t[h][:])

        def fin_amax(h, u):
            nc.vector.tensor_reduce(out=stat[:, 4 * h + u:4 * h + u + 1], in_=osb_t[h][:, 256 * u:256 * u + 256],
                                    axis=AX.X, op=ALU.max, apply_absolute_value=True)

        def fin_scale(h):
            nc.vector.tensor_scalar(out=stat[:, 4 * h + 2:4 * h + 3], in0=stat[:, 4 * h:4 * h + 1],
                                    scalar1=stat[:, 4 * h + 1:4 * h + 2], scalar2=1.0 / 448.0,
                                    op0=ALU.max, op1=ALU.mult)
            nc.vector.reciprocal(out=stat[:, 4 * h + 3:4 * h + 4], in_=stat[:, 4 * h + 2:4 * h + 3])

        def fin_cast(h, vcols):
            o8_t[h] = work.tile([P, CH], FP8, name="o8_%d" % h, tag="o8", bufs=2)
            r = stat[:, 4 * h + 3:4 * h + 4]
            if vcols > 0:
                nc.vector.tensor_scalar(out=o8_t[h][:, 0:vcols], in0=osb_t[h][:, 0:vcols], scalar1=r, scalar2=None,
                                        op0=ALU.mult, saturate=False)
            if vcols < CH:
                nc.scalar.activation(out=o8_t[h][:, vcols:CH], in_=osb_t[h][:, vcols:CH], func=ACT.Identity,
                                     scale=r, bias=zero[:, 0:1], saturate=False)
            nc.sync.dma_start(out=out_1[128 * h:128 * h + 128, :], in_=o8_t[h][:].bitcast(U8))

        warm(NWARM[0])
        uwords = tiles[("u", 0)][:].bitcast(F32)
        ups = []
        for uh in range(2):
            up = psum.tile([P, 4, P], F32, name="up%d" % uh, tag="ct", bufs=2)
            for m in range(4):
                nc.tensor.transpose(up[:, m, :], uwords[:, m // 2, m % 2, 128 * uh:128 * uh + 128], ident[:])
            ups.append(up)
        for uh in range(2):
            v = ups[uh][:].rearrange("p m c -> p (m c)").bitcast(BF16).rearrange("p (x e) -> p e x", e=2)
            if uh == 0:
                nc.vector.tensor_copy(out=ut[:, 0:2, :], in_=v)
            else:
                nc.scalar.copy(out=ut[:, 2:4, :], in_=v)
        warm(NWARM[1])
        ht_a, ops_a = th_ops(0, 0, "ht", 1)
        for op in ops_a:
            emit_t(op)
        ht_b, ops_b = th_ops(0, 1, "q", 1)
        for op in ops_b:
            emit_t(op)
        copy_h(True, 0, 0, ht_a)
        copy_h(False, 0, 1, ht_b)
        released["h"] += 2
        warm(NWARM[2])
        nc.vector.tensor_copy(out=bias[:], in_=bias_bf[:].rearrange("p u e -> p (u e)"))

        pro = []
        for u in range(2):
            for g in range(2):
                pro.append((("w", u), g, wcodes[:, g, 256 * u:256 * u + 256], wscales[:, g, 256 * u:256 * u + 256]))
        for z in range(4):
            cd, sc = z_dest(z)
            pro.append((("zn", z // 2), z % 2, cd, sc))
        qz_list = []
        for pu in range(2):
            z_t = []
            zts = []
            for k in range(4 * pu, 4 * pu + 4):
                zt, ops = quarter_ops(tiles[pro[k][0]], pro[k][1], "pzt%d" % k, ("zt", "ct")[(k % 4) // 2])
                zts.append((k, zt))
                z_t.extend(ops)
            weave([(pu, kt) for kt in range(4)], z_t, [])
            if pu >= 1:
                op_a(pu - 1)
            for item in qz_list:
                quantize(*item)
            qz_list.clear()
            for n_, (k, zt) in enumerate(zts):
                grp = copy_quarter(n_ % 2 == 0, zt, "pgrp%d" % k)
                qz_list.append((grp, pro[k][2], pro[k][3]))
        released["zn"] += 2
        ht10, ops10 = th_ops(1, 0, "q", 1)
        ht11, ops11 = th_ops(1, 1, "ht", 1)
        weave([(2, kt) for kt in range(4)], ops10 + ops11, [])
        op_a(1)
        for item in qz_list:
            quantize(*item)
        qz_list.clear()
        copy_h(True, 1, 0, ht10)
        copy_h(True, 1, 1, ht11)
        released["h"] += 2
        pump()

        zt_list = []
        stream = [(u, kt) for u in range(LP, NSTEP) for kt in range(4)]
        spos = 0
        a_list = [LP - 1]
        for s in range(NSTEP):
            mx(s)
            for u in a_list:
                op_a(u)
            a_list.clear()
            if s >= 1:
                op_sg(s - 1)
            qz_now = list(qz_list)
            qz_list.clear()
            for n_, (z, zt) in enumerate(zt_list):
                grp = copy_quarter(n_ == 0, zt, "grp%d" % z)
                cd, sc = z_dest(z)
                qz_list.append((grp, cd, sc))
            zt_list.clear()
            if s >= 4 and s % 2 == 0:
                op_e_pair(s - 4)
            if s == NSTEP - 1:
                op_e_pair(s - 3)
            op_b(s)
            for item in qz_now:
                quantize(*item)
            if s >= 1:
                op_d(s - 1)
                if s - 1 < NSTEP - 2:
                    op_tree(s - 1)
            z_t = []
            zl = ((4, 5), (6, 7))[s] if s < 2 else ((s + 6,) if s + 6 < NSTEP else ())
            for z in zl:
                zt, ops = z_ops(z)
                zt_list.append((z, zt))
                z_t.extend(ops)
            o_t = []
            ht = None
            gi, jp = (s + 6) // 4, ((s + 6) % 4) // 2
            if s % 2 == 0 and 2 <= gi < NG:
                ht, o_t = th_ops(gi, jp, "ht", 1)
            gc, uc = (s + 1) // 4, ((s + 1) % 4) // 2
            if s % 2 == 1 and gc < NG:
                o_t = tc_ops(gc, uc)
            if s == 0:
                z_t.extend(tc_ops(0, 0))
            upto = min(len(stream), (len(stream) * (s + 1) + NSTEP - 2) // (NSTEP - 1))
            items = stream[spos:upto]
            spos = upto
            weave(items, z_t, o_t)
            if s < 2:
                for n_, (z, zt) in enumerate(zt_list):
                    grp = copy_quarter(n_ == 0, zt, "grp%d" % z)
                    cd, sc = z_dest(z)
                    qz_list.append((grp, cd, sc))
                zt_list.clear()
            for it in items:
                if it[1] == 3:
                    a_list.append(it[0])
            if ht is not None:
                copy_h(False, gi, jp, ht)
                released["h"] += 1
            for z in zl:
                if z % 2 == 1:
                    released["zn"] += 1
            if s % 2 == 1 and gc < NG and uc == 1:
                released["c"] += 2
            pump()

        last = NSTEP - 1
        ft00 = fin_t(0, 0, "zt", 2)
        ft01 = fin_t(0, 1, "zt", 2)
        ft10 = fin_t(1, 0, "ht", 1)
        op_sg(last)
        op_e(last - 1)
        fin_copy(0, 0, ft00)
        fin_copy(0, 1, ft01)
        fin_copy(1, 0, ft10)
        op_d(last)
        fin_amax(0, 0)
        op_e(last)
        ft11 = fin_t(1, 1, "ct", 2)
        fin_copy(1, 1, ft11)
        fin_amax(0, 1)
        fin_scale(0)
        fin_amax(1, 0)
        fin_cast(0, 0)
        fin_amax(1, 1)
        fin_scale(1)
        fin_cast(1, 256)
